import numpy as np
import ml_dtypes

BF16 = ml_dtypes.bfloat16


def bf(x):
    return np.asarray(x, np.float32).astype(BF16)


def f32(x):
    return np.asarray(x, np.float32)


def f64(x):
    return np.asarray(x).astype(np.float64)


def striped(idx):
    return np.tile(idx.reshape(-1, 16).T, (8, 1))


D, S, H, H2, DH, N = 128, 4096, 512, 1024, 64, 2048
QSCALE = DH ** -0.5


def setup_inputs():
    return {
        "table": bf(np.random.standard_normal((D, S))),
        "w": bf(np.random.standard_normal((D, H)) / np.sqrt(D)),
        "b": f32(0.1 * np.random.standard_normal((H, 1))),
        "wq": bf(2.0 * np.random.standard_normal((H, H)) / np.sqrt(H)),
        "bq": f32(0.5 * np.random.standard_normal((H, 1))),
        "wk": bf(np.random.standard_normal((H, H)) / np.sqrt(H)),
        "bk": f32(0.1 * np.random.standard_normal((H, 1))),
        "path_w": bf(np.random.standard_normal((H2, H)) / np.sqrt(H)),
        "offs": striped(np.random.permutation(np.tile(np.arange(S), 2))[:N]),
    }


def reference(table, w, b, wq, bq, wk, bk, path_w, offs):
    idx = offs[:16].T.reshape(-1)
    rel = f64(w).T @ f64(table)[:, idx] + f64(b)
    query = (f64(wq).T @ rel + f64(bq)) * QSCALE
    key = f64(wk).T @ rel + f64(bk)
    pa = f64(path_w)[:H].T @ rel
    pb = f64(path_w)[H:].T @ rel
    return np.concatenate([rel, query, key, pa, pb], axis=0)

@@ -1,0 +1,99 @@
+import concourse.mybir as mybir
+
+F32 = mybir.dt.float32
+BF16 = mybir.dt.bfloat16
+U16 = mybir.dt.uint16
+ADD = mybir.AluOpType.add
+MULT = mybir.AluOpType.mult
+IDENTITY = mybir.ActivationFunctionType.Identity
+
+P = 128
+S = 4096
+H = 512
+N = 2048
+PIECE = 512
+BLOCKS = H // P
+PIECES = N // PIECE
+QSCALE = 0.125
+
+FLOPS = 2 * P * H * N + 4 * 2 * H * H * N
+
+
+def tile_adjmatmulencoder_b_kernel(tc, table, w, b, wq, bq, wk, bk, path_w, offs, out):
+    nc = tc.nc
+    with (
+        tc.tile_pool(name="held", bufs=1) as held,
+        tc.tile_pool(name="stage", bufs=8) as stage,
+        tc.psum_pool(name="psum", bufs=8) as psum,
+    ):
+        offsets = held.tile([P, N // 16], U16, name="offsets")
+        nc.sync.dma_start(offsets[:], offs)
+        w_sb = held.tile([P, H], BF16, name="w_sb")
+        nc.sync.dma_start(w_sb[:], w)
+        table_sb = held.tile([P, S], BF16, name="table_sb")
+        nc.sync.dma_start(table_sb[:], table)
+
+        wq_sb = held.tile([P, BLOCKS, H], BF16, name="wq_sb")
+        nc.sync.dma_start(wq_sb[:], wq.rearrange("(k p) m -> p k m", p=P))
+        wk_sb = held.tile([P, BLOCKS, H], BF16, name="wk_sb")
+        nc.sync.dma_start(wk_sb[:], wk.rearrange("(k p) m -> p k m", p=P))
+        path_sb = held.tile([P, 2 * BLOCKS, H], BF16, name="path_sb")
+        nc.sync.dma_start(path_sb[:], path_w.rearrange("(k p) m -> p k m", p=P))
+
+        b_sb = held.tile([P, BLOCKS], F32, name="b_sb")
+        bq_sb = held.tile([P, BLOCKS], F32, name="bq_sb")
+        bk_sb = held.tile([P, BLOCKS], F32, name="bk_sb")
+        with nc.allow_non_contiguous_dma(reason="three bias vectors, one element to a partition"):
+            nc.scalar.dma_start(b_sb[:], b.rearrange("(m p) o -> p (m o)", p=P))
+            nc.scalar.dma_start(bq_sb[:], bq.rearrange("(m p) o -> p (m o)", p=P))
+            nc.scalar.dma_start(bk_sb[:], bk.rearrange("(m p) o -> p (m o)", p=P))
+
+        def store(section, m, piece, staged):
+            row = section * H + m * P
+            nc.sync.dma_start(out[row : row + P, piece * PIECE : (piece + 1) * PIECE], staged[:])
+
+        rel_bf = [[None] * BLOCKS for piece in range(PIECES)]
+        for piece in range(PIECES):
+            picked = table_sb[:].indirect(offsets[:, piece * (PIECE // 16) : (piece + 1) * (PIECE // 16)])
+            for m in range(BLOCKS):
+                acc = psum.tile([P, PIECE], F32, name="acc")
+                nc.tensor.matmul(acc[:], w_sb[:, m * P : (m + 1) * P], picked, start=True, stop=True)
+                staged = stage.tile([P, PIECE], F32, name="staged")
+                nc.vector.tensor_scalar(staged[:], acc[:], b_sb[:, m : m + 1], None, op0=ADD)
+                rel_bf[piece][m] = held.tile([P, PIECE], BF16, name=f"rel_bf_{piece}_{m}")
+                nc.scalar.copy(rel_bf[piece][m][:], staged[:])
+                store(0, m, piece, staged)
+
+        def project(weights, first_block, m, piece):
+            acc = psum.tile([P, PIECE], F32, name="acc")
+            for k in range(BLOCKS):
+                nc.tensor.matmul(
+                    acc[:],
+                    weights[:, first_block + k, m * P : (m + 1) * P],
+                    rel_bf[piece][k][:],
+                    start=(k == 0),
+                    stop=(k == BLOCKS - 1),
+                )
+            return acc
+
+        for piece in range(PIECES):
+            for m in range(BLOCKS):
+                acc = project(wq_sb, 0, m, piece)
+                staged = stage.tile([P, PIECE], F32, name="staged")
+                nc.vector.tensor_scalar(staged[:], acc[:], bq_sb[:, m : m + 1], QSCALE, op0=ADD, op1=MULT)
+                store(1, m, piece, staged)
+
+                acc = project(wk_sb, 0, m, piece)
+                staged = stage.tile([P, PIECE], F32, name="staged")
+                nc.scalar.activation(staged[:], acc[:], IDENTITY, bias=bk_sb[:, m : m + 1])
+                store(2, m, piece, staged)
+
+                acc = project(path_sb, 0, m, piece)
+                staged = stage.tile([P, PIECE], F32, name="staged")
+                nc.vector.tensor_copy(staged[:], acc[:])
+                store(3, m, piece, staged)
+
+                acc = project(path_sb, BLOCKS, m, piece)
+                staged = stage.tile([P, PIECE], F32, name="staged")
+                nc.scalar.copy(staged[:], acc[:])
+                store(4, m, piece, staged)

@@ -15,6 +15,7 @@ PIECE = 512
 BLOCKS = H // P
 PIECES = N // PIECE
 QSCALE = 0.125
+WARMUP = 10
 
 FLOPS = 2 * P * H * N + 4 * 2 * H * H * N
 
@@ -47,6 +48,12 @@ def tile_adjmatmulencoder_b_kernel(tc, table, w, b, wq, bq, wk, bk, path_w, offs
             nc.scalar.dma_start(b_sb[:], b.rearrange("(m p) o -> p (m o)", p=P))
             nc.scalar.dma_start(bq_sb[:], bq.rearrange("(m p) o -> p (m o)", p=P))
             nc.scalar.dma_start(bk_sb[:], bk.rearrange("(m p) o -> p (m o)", p=P))
+
+        zeros = held.tile([P, PIECE], BF16, name="zeros")
+        nc.vector.memset(zeros[:], 0.0)
+        acc = psum.tile([P, PIECE], F32, name="acc")
+        for i in range(WARMUP):
+            nc.tensor.matmul(acc[:], zeros[:, 0:P], zeros[:], start=True, stop=True)
 
         def store(section, m, piece, staged):
             row = section * H + m * P

@@ -15,7 +15,6 @@ PIECE = 512
 BLOCKS = H // P
 PIECES = N // PIECE
 QSCALE = 0.125
-WARMUP = 10
 
 FLOPS = 2 * P * H * N + 4 * 2 * H * H * N
 
@@ -28,32 +27,24 @@ def tile_adjmatmulencoder_b_kernel(tc, table, w, b, wq, bq, wk, bk, path_w, offs
         tc.psum_pool(name="psum", bufs=8) as psum,
     ):
         offsets = held.tile([P, N // 16], U16, name="offsets")
-        nc.sync.dma_start(offsets[:], offs)
         w_sb = held.tile([P, H], BF16, name="w_sb")
-        nc.sync.dma_start(w_sb[:], w)
         table_sb = held.tile([P, S], BF16, name="table_sb")
-        nc.sync.dma_start(table_sb[:], table)
-
         wq_sb = held.tile([P, BLOCKS, H], BF16, name="wq_sb")
-        nc.sync.dma_start(wq_sb[:], wq.rearrange("(k p) m -> p k m", p=P))
         wk_sb = held.tile([P, BLOCKS, H], BF16, name="wk_sb")
-        nc.sync.dma_start(wk_sb[:], wk.rearrange("(k p) m -> p k m", p=P))
         path_sb = held.tile([P, 2 * BLOCKS, H], BF16, name="path_sb")
-        nc.sync.dma_start(path_sb[:], path_w.rearrange("(k p) m -> p k m", p=P))
-
         b_sb = held.tile([P, BLOCKS], F32, name="b_sb")
         bq_sb = held.tile([P, BLOCKS], F32, name="bq_sb")
         bk_sb = held.tile([P, BLOCKS], F32, name="bk_sb")
+        nc.sync.dma_start(offsets[:], offs)
+        nc.sync.dma_start(w_sb[:], w)
+        nc.sync.dma_start(table_sb[:], table)
         with nc.allow_non_contiguous_dma(reason="three bias vectors, one element to a partition"):
-            nc.scalar.dma_start(b_sb[:], b.rearrange("(m p) o -> p (m o)", p=P))
-            nc.scalar.dma_start(bq_sb[:], bq.rearrange("(m p) o -> p (m o)", p=P))
-            nc.scalar.dma_start(bk_sb[:], bk.rearrange("(m p) o -> p (m o)", p=P))
-
-        zeros = held.tile([P, PIECE], BF16, name="zeros")
-        nc.vector.memset(zeros[:], 0.0)
-        acc = psum.tile([P, PIECE], F32, name="acc")
-        for i in range(WARMUP):
-            nc.tensor.matmul(acc[:], zeros[:, 0:P], zeros[:], start=True, stop=True)
+            nc.sync.dma_start(b_sb[:], b.rearrange("(m p) o -> p (m o)", p=P))
+            nc.sync.dma_start(wq_sb[:], wq.rearrange("(k p) m -> p k m", p=P))
+            nc.sync.dma_start(bq_sb[:], bq.rearrange("(m p) o -> p (m o)", p=P))
+            nc.sync.dma_start(wk_sb[:], wk.rearrange("(k p) m -> p k m", p=P))
+            nc.sync.dma_start(bk_sb[:], bk.rearrange("(m p) o -> p (m o)", p=P))
+            nc.sync.dma_start(path_sb[:], path_w.rearrange("(k p) m -> p k m", p=P))
 
         def store(section, m, piece, staged):
             row = section * H + m * P

@@ -15,6 +15,7 @@ PIECE = 512
 BLOCKS = H // P
 PIECES = N // PIECE
 QSCALE = 0.125
+LAST_SLICES = 4
 
 FLOPS = 2 * P * H * N + 4 * 2 * H * H * N
 
@@ -46,9 +47,9 @@ def tile_adjmatmulencoder_b_kernel(tc, table, w, b, wq, bq, wk, bk, path_w, offs
             nc.sync.dma_start(bk_sb[:], bk.rearrange("(m p) o -> p (m o)", p=P))
             nc.sync.dma_start(path_sb[:], path_w.rearrange("(k p) m -> p k m", p=P))
 
-        def store(section, m, piece, staged):
+        def store(section, m, first_col, staged):
             row = section * H + m * P
-            nc.sync.dma_start(out[row : row + P, piece * PIECE : (piece + 1) * PIECE], staged[:])
+            nc.sync.dma_start(out[row : row + P, first_col : first_col + staged.shape[1]], staged)
 
         rel_bf = [[None] * BLOCKS for piece in range(PIECES)]
         for piece in range(PIECES):
@@ -60,15 +61,15 @@ def tile_adjmatmulencoder_b_kernel(tc, table, w, b, wq, bq, wk, bk, path_w, offs
                 nc.vector.tensor_scalar(staged[:], acc[:], b_sb[:, m : m + 1], None, op0=ADD)
                 rel_bf[piece][m] = held.tile([P, PIECE], BF16, name=f"rel_bf_{piece}_{m}")
                 nc.scalar.copy(rel_bf[piece][m][:], staged[:])
-                store(0, m, piece, staged)
+                store(0, m, piece * PIECE, staged[:])
 
-        def project(weights, first_block, m, piece):
-            acc = psum.tile([P, PIECE], F32, name="acc")
+        def project(weights, first_block, m, piece, first=0, cols=PIECE):
+            acc = psum.tile([P, cols], F32, name="acc")
             for k in range(BLOCKS):
                 nc.tensor.matmul(
                     acc[:],
                     weights[:, first_block + k, m * P : (m + 1) * P],
-                    rel_bf[piece][k][:],
+                    rel_bf[piece][k][:, first : first + cols],
                     start=(k == 0),
                     stop=(k == BLOCKS - 1),
                 )
@@ -79,19 +80,25 @@ def tile_adjmatmulencoder_b_kernel(tc, table, w, b, wq, bq, wk, bk, path_w, offs
                 acc = project(wq_sb, 0, m, piece)
                 staged = stage.tile([P, PIECE], F32, name="staged")
                 nc.vector.tensor_scalar(staged[:], acc[:], bq_sb[:, m : m + 1], QSCALE, op0=ADD, op1=MULT)
-                store(1, m, piece, staged)
+                store(1, m, piece * PIECE, staged[:])
 
                 acc = project(wk_sb, 0, m, piece)
                 staged = stage.tile([P, PIECE], F32, name="staged")
                 nc.scalar.activation(staged[:], acc[:], IDENTITY, bias=bk_sb[:, m : m + 1])
-                store(2, m, piece, staged)
+                store(2, m, piece * PIECE, staged[:])
 
                 acc = project(path_sb, 0, m, piece)
                 staged = stage.tile([P, PIECE], F32, name="staged")
                 nc.vector.tensor_copy(staged[:], acc[:])
-                store(3, m, piece, staged)
+                store(3, m, piece * PIECE, staged[:])
 
-                acc = project(path_sb, BLOCKS, m, piece)
-                staged = stage.tile([P, PIECE], F32, name="staged")
-                nc.scalar.copy(staged[:], acc[:])
-                store(4, m, piece, staged)
+                last = piece == PIECES - 1 and m == BLOCKS - 1
+                cols = PIECE // LAST_SLICES if last else PIECE
+                for first in range(0, PIECE, cols):
+                    acc = project(path_sb, BLOCKS, m, piece, first, cols)
+                    staged = stage.tile([P, cols], F32, name="staged")
+                    if (first // cols) % 2 == 0:
+                        nc.scalar.copy(staged[:], acc[:])
+                    else:
+                        nc.vector.tensor_copy(staged[:], acc[:])
+                    store(4, m, piece * PIECE + first, staged[:])

@@ -37,9 +37,10 @@ def tile_adjmatmulencoder_b_kernel(tc, table, w, b, wq, bq, wk, bk, path_w, offs
         bq_sb = held.tile([P, BLOCKS], F32, name="bq_sb")
         bk_sb = held.tile([P, BLOCKS], F32, name="bk_sb")
         nc.sync.dma_start(offsets[:], offs)
-        nc.sync.dma_start(w_sb[:], w)
-        nc.sync.dma_start(table_sb[:], table)
-        with nc.allow_non_contiguous_dma(reason="three bias vectors, one element to a partition"):
+        with nc.allow_non_contiguous_dma(reason="column blocks of w; three bias vectors, one element to a partition"):
+            nc.sync.dma_start(w_sb[:, 0:P], w[:, 0:P])
+            nc.sync.dma_start(table_sb[:], table)
+            nc.sync.dma_start(w_sb[:, P:H], w[:, P:H])
             nc.sync.dma_start(b_sb[:], b.rearrange("(m p) o -> p (m o)", p=P))
             nc.sync.dma_start(wq_sb[:], wq.rearrange("(k p) m -> p k m", p=P))
             nc.sync.dma_start(bq_sb[:], bq.rearrange("(m p) o -> p (m o)", p=P))

@@ -39,7 +39,8 @@ def tile_adjmatmulencoder_b_kernel(tc, table, w, b, wq, bq, wk, bk, path_w, offs
         nc.sync.dma_start(offsets[:], offs)
         with nc.allow_non_contiguous_dma(reason="column blocks of w; three bias vectors, one element to a partition"):
             nc.sync.dma_start(w_sb[:, 0:P], w[:, 0:P])
-            nc.sync.dma_start(table_sb[:], table)
+            nc.sync.dma_start(table_sb[:, 0 : S // 2], table[:, 0 : S // 2])
+            nc.scalar.dma_start(table_sb[:, S // 2 : S], table[:, S // 2 : S])
             nc.sync.dma_start(w_sb[:, P:H], w[:, P:H])
             nc.sync.dma_start(b_sb[:], b.rearrange("(m p) o -> p (m o)", p=P))
             nc.sync.dma_start(wq_sb[:], wq.rearrange("(k p) m -> p k m", p=P))

@@ -54,7 +54,8 @@ def tile_adjmatmulencoder_b_kernel(tc, table, w, b, wq, bq, wk, bk, path_w, offs
             nc.sync.dma_start(out[row : row + P, first_col : first_col + staged.shape[1]], staged)
 
         rel_bf = [[None] * BLOCKS for piece in range(PIECES)]
-        for piece in range(PIECES):
+
+        def look_up(piece):
             picked = table_sb[:].indirect(offsets[:, piece * (PIECE // 16) : (piece + 1) * (PIECE // 16)])
             for m in range(BLOCKS):
                 acc = psum.tile([P, PIECE], F32, name="acc")
@@ -77,7 +78,10 @@ def tile_adjmatmulencoder_b_kernel(tc, table, w, b, wq, bq, wk, bk, path_w, offs
                 )
             return acc
 
+        look_up(0)
         for piece in range(PIECES):
+            if piece + 1 < PIECES:
+                look_up(piece + 1)
             for m in range(BLOCKS):
                 acc = project(wq_sb, 0, m, piece)
                 staged = stage.tile([P, PIECE], F32, name="staged")

@@ -32,7 +32,8 @@ def tile_adjmatmulencoder_b_kernel(tc, table, w, b, wq, bq, wk, bk, path_w, offs
         table_sb = held.tile([P, S], BF16, name="table_sb")
         wq_sb = held.tile([P, BLOCKS, H], BF16, name="wq_sb")
         wk_sb = held.tile([P, BLOCKS, H], BF16, name="wk_sb")
-        path_sb = held.tile([P, 2 * BLOCKS, H], BF16, name="path_sb")
+        pa_sb = held.tile([P, BLOCKS, H], BF16, name="pa_sb")
+        pb_sb = held.tile([P, BLOCKS, H], BF16, name="pb_sb")
         b_sb = held.tile([P, BLOCKS], F32, name="b_sb")
         bq_sb = held.tile([P, BLOCKS], F32, name="bq_sb")
         bk_sb = held.tile([P, BLOCKS], F32, name="bk_sb")
@@ -44,10 +45,11 @@ def tile_adjmatmulencoder_b_kernel(tc, table, w, b, wq, bq, wk, bk, path_w, offs
             nc.sync.dma_start(w_sb[:, P:H], w[:, P:H])
             nc.sync.dma_start(b_sb[:], b.rearrange("(m p) o -> p (m o)", p=P))
             nc.sync.dma_start(wq_sb[:], wq.rearrange("(k p) m -> p k m", p=P))
-            nc.sync.dma_start(bq_sb[:], bq.rearrange("(m p) o -> p (m o)", p=P))
             nc.sync.dma_start(wk_sb[:], wk.rearrange("(k p) m -> p k m", p=P))
+            nc.sync.dma_start(pa_sb[:], path_w[0:H, :].rearrange("(k p) m -> p k m", p=P))
+            nc.sync.dma_start(pb_sb[:], path_w[H : 2 * H, :].rearrange("(k p) m -> p k m", p=P))
+            nc.sync.dma_start(bq_sb[:], bq.rearrange("(m p) o -> p (m o)", p=P))
             nc.sync.dma_start(bk_sb[:], bk.rearrange("(m p) o -> p (m o)", p=P))
-            nc.sync.dma_start(path_sb[:], path_w.rearrange("(k p) m -> p k m", p=P))
 
         def store(section, m, first_col, staged):
             row = section * H + m * P
@@ -93,7 +95,7 @@ def tile_adjmatmulencoder_b_kernel(tc, table, w, b, wq, bq, wk, bk, path_w, offs
                 nc.scalar.activation(staged[:], acc[:], IDENTITY, bias=bk_sb[:, m : m + 1])
                 store(2, m, piece * PIECE, staged[:])
 
-                acc = project(path_sb, 0, m, piece)
+                acc = project(pa_sb, 0, m, piece)
                 staged = stage.tile([P, PIECE], F32, name="staged")
                 nc.vector.tensor_copy(staged[:], acc[:])
                 store(3, m, piece * PIECE, staged[:])
@@ -101,7 +103,7 @@ def tile_adjmatmulencoder_b_kernel(tc, table, w, b, wq, bq, wk, bk, path_w, offs
                 last = piece == PIECES - 1 and m == BLOCKS - 1
                 cols = PIECE // LAST_SLICES if last else PIECE
                 for first in range(0, PIECE, cols):
-                    acc = project(path_sb, BLOCKS, m, piece, first, cols)
+                    acc = project(pb_sb, 0, m, piece, first, cols)
                     staged = stage.tile([P, cols], F32, name="staged")
                     if (first // cols) % 2 == 0:
                         nc.scalar.copy(staged[:], acc[:])

@@ -57,9 +57,9 @@ def tile_adjmatmulencoder_b_kernel(tc, table, w, b, wq, bq, wk, bk, path_w, offs
 
         rel_bf = [[None] * BLOCKS for piece in range(PIECES)]
 
-        def look_up(piece):
+        def look_up(piece, blocks):
             picked = table_sb[:].indirect(offsets[:, piece * (PIECE // 16) : (piece + 1) * (PIECE // 16)])
-            for m in range(BLOCKS):
+            for m in blocks:
                 acc = psum.tile([P, PIECE], F32, name="acc")
                 nc.tensor.matmul(acc[:], w_sb[:, m * P : (m + 1) * P], picked, start=True, stop=True)
                 staged = stage.tile([P, PIECE], F32, name="staged")
@@ -80,11 +80,11 @@ def tile_adjmatmulencoder_b_kernel(tc, table, w, b, wq, bq, wk, bk, path_w, offs
                 )
             return acc
 
-        look_up(0)
+        look_up(0, range(BLOCKS))
         for piece in range(PIECES):
-            if piece + 1 < PIECES:
-                look_up(piece + 1)
             for m in range(BLOCKS):
+                if piece + 1 < PIECES and m % 2 == 0:
+                    look_up(piece + 1, (m, m + 1))
                 acc = project(wq_sb, 0, m, piece)
                 staged = stage.tile([P, PIECE], F32, name="staged")
                 nc.vector.tensor_scalar(staged[:], acc[:], bq_sb[:, m : m + 1], QSCALE, op0=ADD, op1=MULT)

@@ -15,7 +15,8 @@ PIECE = 512
 BLOCKS = H // P
 PIECES = N // PIECE
 QSCALE = 0.125
-LAST_SLICES = 4
+PA_LAST = PIECE // 2
+PB_LAST = PIECE // 4
 
 FLOPS = 2 * P * H * N + 4 * 2 * H * H * N
 
@@ -95,18 +96,13 @@ def tile_adjmatmulencoder_b_kernel(tc, table, w, b, wq, bq, wk, bk, path_w, offs
                 nc.scalar.activation(staged[:], acc[:], IDENTITY, bias=bk_sb[:, m : m + 1])
                 store(2, m, piece * PIECE, staged[:])
 
-                acc = project(pa_sb, 0, m, piece)
-                staged = stage.tile([P, PIECE], F32, name="staged")
-                nc.vector.tensor_copy(staged[:], acc[:])
-                store(3, m, piece * PIECE, staged[:])
-
                 last = piece == PIECES - 1 and m == BLOCKS - 1
-                cols = PIECE // LAST_SLICES if last else PIECE
-                for first in range(0, PIECE, cols):
-                    acc = project(pb_sb, 0, m, piece, first, cols)
-                    staged = stage.tile([P, cols], F32, name="staged")
-                    if (first // cols) % 2 == 0:
-                        nc.scalar.copy(staged[:], acc[:])
-                    else:
-                        nc.vector.tensor_copy(staged[:], acc[:])
-                    store(4, m, piece * PIECE + first, staged[:])
+                for weights, section, cols in ((pa_sb, 3, PA_LAST if last else PIECE), (pb_sb, 4, PB_LAST if last else PIECE)):
+                    for first in range(0, PIECE, cols):
+                        acc = project(weights, 0, m, piece, first, cols)
+                        staged = stage.tile([P, cols], F32, name="staged")
+                        if (section + first // cols) % 2 == 0:
+                            nc.scalar.copy(staged[:], acc[:])
+                        else:
+                            nc.vector.tensor_copy(staged[:], acc[:])
+                        store(section, m, piece * PIECE + first, staged[:])

@@ -1,4 +1,5 @@
 import concourse.mybir as mybir
+from concourse.masks import make_identity
 
 F32 = mybir.dt.float32
 BF16 = mybir.dt.bfloat16
@@ -35,22 +36,30 @@ def tile_adjmatmulencoder_b_kernel(tc, table, w, b, wq, bq, wk, bk, path_w, offs
         wk_sb = held.tile([P, BLOCKS, H], BF16, name="wk_sb")
         pa_sb = held.tile([P, BLOCKS, H], BF16, name="pa_sb")
         pb_sb = held.tile([P, BLOCKS, H], BF16, name="pb_sb")
-        b_sb = held.tile([P, BLOCKS], F32, name="b_sb")
-        bq_sb = held.tile([P, BLOCKS], F32, name="bq_sb")
-        bk_sb = held.tile([P, BLOCKS], F32, name="bk_sb")
+        biases = held.tile([P, 3 * BLOCKS], F32, name="biases")
+        b_sb = biases[:, 0:BLOCKS]
+        bq_sb = biases[:, BLOCKS : 2 * BLOCKS]
+        bk_sb = biases[:, 2 * BLOCKS : 3 * BLOCKS]
         nc.sync.dma_start(offsets[:], offs)
-        with nc.allow_non_contiguous_dma(reason="column blocks of w; three bias vectors, one element to a partition"):
+        bias_rows = held.tile([P, P], F32, name="bias_rows")
+        nc.vector.memset(bias_rows[:], 0.0)
+        with nc.allow_non_contiguous_dma(reason="column blocks of w"):
             nc.sync.dma_start(w_sb[:, 0:P], w[:, 0:P])
-            nc.sync.dma_start(table_sb[:, 0 : S // 2], table[:, 0 : S // 2])
+            for i, bias in enumerate((b, bq, bk)):
+                nc.sync.dma_start(bias_rows[i * BLOCKS : (i + 1) * BLOCKS, :], bias.rearrange("(m p) o -> m (p o)", p=P))
             nc.scalar.dma_start(table_sb[:, S // 2 : S], table[:, S // 2 : S])
+            nc.sync.dma_start(table_sb[:, 0 : S // 2], table[:, 0 : S // 2])
             nc.sync.dma_start(w_sb[:, P:H], w[:, P:H])
-            nc.sync.dma_start(b_sb[:], b.rearrange("(m p) o -> p (m o)", p=P))
             nc.sync.dma_start(wq_sb[:], wq.rearrange("(k p) m -> p k m", p=P))
             nc.sync.dma_start(wk_sb[:], wk.rearrange("(k p) m -> p k m", p=P))
             nc.sync.dma_start(pa_sb[:], path_w[0:H, :].rearrange("(k p) m -> p k m", p=P))
             nc.sync.dma_start(pb_sb[:], path_w[H : 2 * H, :].rearrange("(k p) m -> p k m", p=P))
-            nc.sync.dma_start(bq_sb[:], bq.rearrange("(m p) o -> p (m o)", p=P))
-            nc.sync.dma_start(bk_sb[:], bk.rearrange("(m p) o -> p (m o)", p=P))
+
+        identity = held.tile([P, P], F32, name="identity")
+        make_identity(nc, identity[:])
+        flipped = psum.tile([P, P], F32, name="flipped", tag="acc")
+        nc.tensor.transpose(flipped[:], bias_rows[:], identity[:])
+        nc.vector.tensor_copy(biases[:], flipped[:, 0 : 3 * BLOCKS])
 
         def store(section, m, first_col, staged):
             row = section * H + m * P

@@ -57,9 +57,9 @@ def tile_adjmatmulencoder_b_kernel(tc, table, w, b, wq, bq, wk, bk, path_w, offs
 
         identity = held.tile([P, P], F32, name="identity")
         make_identity(nc, identity[:])
-        flipped = psum.tile([P, P], F32, name="flipped", tag="acc")
-        nc.tensor.transpose(flipped[:], bias_rows[:], identity[:])
-        nc.vector.tensor_copy(biases[:], flipped[:, 0 : 3 * BLOCKS])
+        flipped = psum.tile([P, 3 * BLOCKS], F32, name="flipped", tag="acc")
+        nc.tensor.matmul(flipped[:], bias_rows[:], identity[:, 0 : 3 * BLOCKS], start=True, stop=True)
+        nc.vector.tensor_copy(biases[:], flipped[:])
 
         def store(section, m, first_col, staged):
             row = section * H + m * P

@@ -16,8 +16,7 @@ PIECE = 512
 BLOCKS = H // P
 PIECES = N // PIECE
 QSCALE = 0.125
-PA_LAST = PIECE // 2
-PB_LAST = PIECE // 4
+LAST_COLS = (PIECE, PIECE, PIECE // 2, PIECE // 4)
 
 FLOPS = 2 * P * H * N + 4 * 2 * H * H * N
 
@@ -78,40 +77,58 @@ def tile_adjmatmulencoder_b_kernel(tc, table, w, b, wq, bq, wk, bk, path_w, offs
                 nc.scalar.copy(rel_bf[piece][m][:], staged[:])
                 store(0, m, piece * PIECE, staged[:])
 
-        def project(weights, first_block, m, piece, first=0, cols=PIECE):
+        def project(weights, m, piece, first=0, cols=PIECE):
             acc = psum.tile([P, cols], F32, name="acc")
             for k in range(BLOCKS):
                 nc.tensor.matmul(
                     acc[:],
-                    weights[:, first_block + k, m * P : (m + 1) * P],
+                    weights[:, k, m * P : (m + 1) * P],
                     rel_bf[piece][k][:, first : first + cols],
                     start=(k == 0),
                     stop=(k == BLOCKS - 1),
                 )
             return acc
 
-        look_up(0, range(BLOCKS))
-        for piece in range(PIECES):
+        def project_query(piece):
             for m in range(BLOCKS):
-                if piece + 1 < PIECES and m % 2 == 0:
-                    look_up(piece + 1, (m, m + 1))
-                acc = project(wq_sb, 0, m, piece)
+                acc = project(wq_sb, m, piece)
                 staged = stage.tile([P, PIECE], F32, name="staged")
                 nc.vector.tensor_scalar(staged[:], acc[:], bq_sb[:, m : m + 1], QSCALE, op0=ADD, op1=MULT)
                 store(1, m, piece * PIECE, staged[:])
 
-                acc = project(wk_sb, 0, m, piece)
+        def project_key(piece):
+            for m in range(BLOCKS):
+                acc = project(wk_sb, m, piece)
                 staged = stage.tile([P, PIECE], F32, name="staged")
                 nc.scalar.activation(staged[:], acc[:], IDENTITY, bias=bk_sb[:, m : m + 1])
                 store(2, m, piece * PIECE, staged[:])
 
-                last = piece == PIECES - 1 and m == BLOCKS - 1
-                for weights, section, cols in ((pa_sb, 3, PA_LAST if last else PIECE), (pb_sb, 4, PB_LAST if last else PIECE)):
-                    for first in range(0, PIECE, cols):
-                        acc = project(weights, 0, m, piece, first, cols)
-                        staged = stage.tile([P, cols], F32, name="staged")
-                        if (section + first // cols) % 2 == 0:
-                            nc.scalar.copy(staged[:], acc[:])
-                        else:
-                            nc.vector.tensor_copy(staged[:], acc[:])
-                        store(section, m, piece * PIECE + first, staged[:])
+        def project_pa(piece):
+            for m in range(BLOCKS):
+                acc = project(pa_sb, m, piece)
+                staged = stage.tile([P, PIECE], F32, name="staged")
+                nc.vector.tensor_copy(staged[:], acc[:])
+                store(3, m, piece * PIECE, staged[:])
+
+        def project_pb(piece):
+            for m in range(BLOCKS):
+                cols = LAST_COLS[m] if piece == PIECES - 1 else PIECE
+                for first in range(0, PIECE, cols):
+                    acc = project(pb_sb, m, piece, first, cols)
+                    staged = stage.tile([P, cols], F32, name="staged")
+                    if (first // cols) % 2 == 0:
+                        nc.scalar.copy(staged[:], acc[:])
+                    else:
+                        nc.vector.tensor_copy(staged[:], acc[:])
+                    store(4, m, piece * PIECE + first, staged[:])
+
+        look_up(0, range(BLOCKS))
+        for piece in range(PIECES):
+            if piece + 1 < PIECES:
+                look_up(piece + 1, (0, 1))
+            project_query(piece)
+            project_key(piece)
+            if piece + 1 < PIECES:
+                look_up(piece + 1, (2, 3))
+            project_pa(piece)
+            project_pb(piece)

import concourse.mybir as mybir
from concourse.masks import make_identity

F32 = mybir.dt.float32
BF16 = mybir.dt.bfloat16
U16 = mybir.dt.uint16
ADD = mybir.AluOpType.add
MULT = mybir.AluOpType.mult
IDENTITY = mybir.ActivationFunctionType.Identity

P = 128
S = 4096
H = 512
N = 2048
PIECE = 512
BLOCKS = H // P
PIECES = N // PIECE
QSCALE = 0.125
LAST_COLS = (PIECE, PIECE, PIECE // 2, PIECE // 4)

FLOPS = 2 * P * H * N + 4 * 2 * H * H * N


def tile_adjmatmulencoder_b_kernel(tc, table, w, b, wq, bq, wk, bk, path_w, offs, out):
    nc = tc.nc
    with (
        tc.tile_pool(name="held", bufs=1) as held,
        tc.tile_pool(name="stage", bufs=8) as stage,
        tc.psum_pool(name="psum", bufs=8) as psum,
    ):
        offsets = held.tile([P, N // 16], U16, name="offsets")
        w_sb = held.tile([P, H], BF16, name="w_sb")
        table_sb = held.tile([P, S], BF16, name="table_sb")
        wq_sb = held.tile([P, BLOCKS, H], BF16, name="wq_sb")
        wk_sb = held.tile([P, BLOCKS, H], BF16, name="wk_sb")
        pa_sb = held.tile([P, BLOCKS, H], BF16, name="pa_sb")
        pb_sb = held.tile([P, BLOCKS, H], BF16, name="pb_sb")
        biases = held.tile([P, 3 * BLOCKS], F32, name="biases")
        b_sb = biases[:, 0:BLOCKS]
        bq_sb = biases[:, BLOCKS : 2 * BLOCKS]
        bk_sb = biases[:, 2 * BLOCKS : 3 * BLOCKS]
        nc.sync.dma_start(offsets[:], offs)
        bias_rows = held.tile([P, P], F32, name="bias_rows")
        nc.vector.memset(bias_rows[:], 0.0)
        with nc.allow_non_contiguous_dma(reason="column blocks of w"):
            nc.sync.dma_start(w_sb[:, 0:P], w[:, 0:P])
            for i, bias in enumerate((b, bq, bk)):
                nc.sync.dma_start(bias_rows[i * BLOCKS : (i + 1) * BLOCKS, :], bias.rearrange("(m p) o -> m (p o)", p=P))
            nc.scalar.dma_start(table_sb[:, S // 2 : S], table[:, S // 2 : S])
            nc.sync.dma_start(table_sb[:, 0 : S // 2], table[:, 0 : S // 2])
            nc.sync.dma_start(w_sb[:, P:H], w[:, P:H])
            nc.sync.dma_start(wq_sb[:], wq.rearrange("(k p) m -> p k m", p=P))
            nc.sync.dma_start(wk_sb[:], wk.rearrange("(k p) m -> p k m", p=P))
            nc.sync.dma_start(pa_sb[:], path_w[0:H, :].rearrange("(k p) m -> p k m", p=P))
            nc.sync.dma_start(pb_sb[:], path_w[H : 2 * H, :].rearrange("(k p) m -> p k m", p=P))

        identity = held.tile([P, P], F32, name="identity")
        make_identity(nc, identity[:])
        flipped = psum.tile([P, 3 * BLOCKS], F32, name="flipped", tag="acc")
        nc.tensor.matmul(flipped[:], bias_rows[:], identity[:, 0 : 3 * BLOCKS], start=True, stop=True)
        nc.vector.tensor_copy(biases[:], flipped[:])

        def store(section, m, first_col, staged):
            row = section * H + m * P
            nc.sync.dma_start(out[row : row + P, first_col : first_col + staged.shape[1]], staged)

        rel_bf = [[None] * BLOCKS for piece in range(PIECES)]

        def look_up(piece, blocks):
            picked = table_sb[:].indirect(offsets[:, piece * (PIECE // 16) : (piece + 1) * (PIECE // 16)])
            for m in blocks:
                acc = psum.tile([P, PIECE], F32, name="acc")
                nc.tensor.matmul(acc[:], w_sb[:, m * P : (m + 1) * P], picked, start=True, stop=True)
                staged = stage.tile([P, PIECE], F32, name="staged")
                nc.vector.tensor_scalar(staged[:], acc[:], b_sb[:, m : m + 1], None, op0=ADD)
                rel_bf[piece][m] = held.tile([P, PIECE], BF16, name=f"rel_bf_{piece}_{m}")
                nc.scalar.copy(rel_bf[piece][m][:], staged[:])
                store(0, m, piece * PIECE, staged[:])

        def project(weights, m, piece, first=0, cols=PIECE):
            acc = psum.tile([P, cols], F32, name="acc")
            for k in range(BLOCKS):
                nc.tensor.matmul(
                    acc[:],
                    weights[:, k, m * P : (m + 1) * P],
                    rel_bf[piece][k][:, first : first + cols],
                    start=(k == 0),
                    stop=(k == BLOCKS - 1),
                )
            return acc

        def project_query(piece):
            for m in range(BLOCKS):
                acc = project(wq_sb, m, piece)
                staged = stage.tile([P, PIECE], F32, name="staged")
                nc.vector.tensor_scalar(staged[:], acc[:], bq_sb[:, m : m + 1], QSCALE, op0=ADD, op1=MULT)
                store(1, m, piece * PIECE, staged[:])

        def project_key(piece):
            for m in range(BLOCKS):
                acc = project(wk_sb, m, piece)
                staged = stage.tile([P, PIECE], F32, name="staged")
                nc.scalar.activation(staged[:], acc[:], IDENTITY, bias=bk_sb[:, m : m + 1])
                store(2, m, piece * PIECE, staged[:])

        def project_pa(piece):
            for m in range(BLOCKS):
                acc = project(pa_sb, m, piece)
                staged = stage.tile([P, PIECE], F32, name="staged")
                nc.vector.tensor_copy(staged[:], acc[:])
                store(3, m, piece * PIECE, staged[:])

        def project_pb(piece):
            for m in range(BLOCKS):
                cols = LAST_COLS[m] if piece == PIECES - 1 else PIECE
                for first in range(0, PIECE, cols):
                    acc = project(pb_sb, m, piece, first, cols)
                    staged = stage.tile([P, cols], F32, name="staged")
                    if (first // cols) % 2 == 0:
                        nc.scalar.copy(staged[:], acc[:])
                    else:
                        nc.vector.tensor_copy(staged[:], acc[:])
                    store(4, m, piece * PIECE + first, staged[:])

        look_up(0, range(BLOCKS))
        for piece in range(PIECES):
            if piece + 1 < PIECES:
                look_up(piece + 1, (0, 1))
            project_query(piece)
            project_key(piece)
            if piece + 1 < PIECES:
                look_up(piece + 1, (2, 3))
            project_pa(piece)
            project_pb(piece)
